import numpy as np
import ml_dtypes


def mxq(x, axis, fmt="e4m3"):
    dtype, down = {"e4m3": (ml_dtypes.float8_e4m3fn, 7), "e5m2": (ml_dtypes.float8_e5m2, 14)}[fmt]
    v = np.moveaxis(np.asarray(x, np.float32).astype(ml_dtypes.bfloat16).astype(np.float64), axis, -1)
    blocks = v.reshape(v.shape[:-1] + (-1, 32))
    amax = np.abs(blocks).max(-1, keepdims=True)
    byte = np.maximum(np.where(amax > 0, np.frexp(amax)[1] - 1 + 127, 0) - down, 1)
    scale = np.exp2(byte - 127.0)
    codes = (blocks / scale).astype(np.float32).astype(dtype).astype(np.float64)
    return np.moveaxis((codes * scale).reshape(v.shape), -1, axis)


WIDE = False


def mx_kscale(k):
    if not WIDE:
        return np.ones(k)
    levels = np.array([10, -10, 5, -5, 0])
    a = np.random.permutation(np.resize(levels, k // 512 * 4)).reshape(k // 512, 4)
    idx = np.arange(k)
    return np.exp2(a[idx // 512, idx % 128 // 32])


BF16 = ml_dtypes.bfloat16


def bf(x):
    return np.asarray(x, np.float32).astype(BF16)


def f64(x):
    return np.asarray(x).astype(np.float64)


B, C, O, H, W, KH, KW, PAD = 2, 512, 256, 8, 8, 3, 3, 1
C_CURV = 0.01
EPS = 1e-7


def artanh(z):
    return 0.5 * np.log((1.0 + z) / (1.0 - z))


def log0(y):
    sqc = np.sqrt(C_CURV)
    n = np.maximum(np.sqrt((y * y).sum(-1, keepdims=True)), EPS)
    return artanh(np.clip(sqc * n, 0.0, 1.0 - 1e-6)) * y / (sqc * n)


def exp0(v):
    sqc = np.sqrt(C_CURV)
    n = np.maximum(np.sqrt((v * v).sum(-1, keepdims=True)), EPS)
    return np.tanh(sqc * n) * v / (sqc * n)


def setup_inputs():
    s = mx_kscale(C)
    rho = np.sqrt(np.mean(s * s))
    raw = np.random.uniform(0.0, 1.0, (B, C, H, W)) * s[None, :, None, None]
    r = np.random.uniform(0.2, 0.85, (B, 1, H, W))
    x = raw / np.sqrt((raw * raw).sum(1, keepdims=True)) * r / np.sqrt(C_CURV)
    return {"x": bf(x),
            "Wk": bf(np.random.standard_normal((KH * KW, O, C)) * 2.1 / np.sqrt(KH * KW * O) * rho / s),
            "bias": bf(np.random.standard_normal(O) * 5.0 / np.sqrt(O))}


def reference(x, Wk, bias):
    Hout, Wout = H + 2 * PAD - KH + 1, W + 2 * PAD - KW + 1
    u = log0(np.moveaxis(f64(x), 1, -1)).reshape(B * H * W, C)
    w = f64(Wk).transpose(2, 0, 1).reshape(C, KH * KW * O)
    y = mxq(u, 1, "e4m3") @ mxq(w, 0, "e4m3")
    yp = np.pad(y.reshape(B, H, W, KH * KW, O), ((0, 0), (PAD, PAD), (PAD, PAD), (0, 0), (0, 0)))
    v = sum(yp[:, i:i + Hout, j:j + Wout, KW * i + j, :] for i in range(KH) for j in range(KW))
    v = np.maximum(v + f64(bias), 0.0)
    out = exp0(v)
    return np.transpose(out, (0, 3, 1, 2))

@@ -1,0 +1,238 @@
+from concourse import mybir
+from concourse.masks import make_identity
+
+F32 = mybir.dt.float32
+BF16 = mybir.dt.bfloat16
+U8 = mybir.dt.uint8
+U32 = mybir.dt.uint32
+I32 = mybir.dt.int32
+FP8X4 = mybir.dt.float8_e4m3fn_x4
+ACT = mybir.ActivationFunctionType
+ALU = mybir.AluOpType
+
+P = 128
+BATCH, CH_IN, CH_OUT, ROWS, COLS = 2, 512, 256, 8, 8
+TAPS = 3
+POSITIONS = TAPS * TAPS
+IMAGE = ROWS * COLS
+PIXELS = BATCH * IMAGE
+PACK = 4
+HALVES = CH_OUT // P
+
+ROW_STEP = BATCH * COLS
+PLANE = (ROWS + 2) * ROW_STEP
+PAD_COLS = 512
+
+SQRT_C = 0.1
+EPS = 1e-7
+FLOPS = 2 * PIXELS * CH_IN * POSITIONS * CH_OUT
+
+
+def tile_pvconv2d_s_kernel(tc, x, Wk, bias, out):
+    nc = tc.nc
+    with (
+        tc.tile_pool(name="keep", bufs=1) as keep,
+        tc.tile_pool(name="small", bufs=1) as small,
+        tc.tile_pool(name="w_in", bufs=POSITIONS) as w_in,
+        tc.tile_pool(name="w_stage", bufs=3) as w_stage,
+        tc.psum_pool(name="ps_w", bufs=4) as ps_w,
+        tc.psum_pool(name="ps_acc", bufs=1) as ps_acc,
+        tc.psum_pool(name="ps_misc", bufs=3) as ps_misc,
+        tc.manual_schedule(),
+    ):
+        x_sb = keep.tile([P, PACK, PIXELS], BF16)
+        x_by_t = x.rearrange("b (u q e) r s -> u e q b (r s)", u=2, q=P, e=2)
+        for t in range(PACK):
+            nc.sync.dma_start(
+                out=x_sb[:, t, :].rearrange("q (b p) -> q b p", b=BATCH), in_=x_by_t[t // 2, t % 2]
+            )
+        w_rows = []
+        for k in range(POSITIONS):
+            rows = w_in.tile([P, HALVES * CH_IN], BF16, name="w_rows")
+            nc.sync.dma_start(out=rows, in_=Wk[k].rearrange("(m h) c -> m (h c)", h=HALVES))
+            w_rows.append(rows)
+        bias_bf = small.tile([P, HALVES], BF16)
+        nc.scalar.dma_start(out=bias_bf, in_=bias.rearrange("(m h) -> m h", h=HALVES))
+
+        one = small.tile([P, 1], F32)
+        nc.vector.memset(one, 1.0)
+        neg_half = small.tile([P, 1], F32)
+        nc.vector.memset(neg_half, -0.5)
+        warm = small.tile([P, 1], F32)
+        nc.scalar.activation(out=warm, in_=one, func=ACT.Ln)
+        ident = keep.tile([P, P], F32)
+        make_identity(nc, ident)
+
+        u_pad = keep.tile([P, PAD_COLS, PACK], BF16, align_bytes=64)
+        nc.vector.memset(u_pad, 0.0)
+        u_codes = keep.tile([P, PAD_COLS], U32, align_bytes=64)
+        u_scales_raw = keep.tile([P, PAD_COLS], U8, align_bytes=64)
+        nc.vector.memset(u_scales_raw.bitcast(I32), 0)
+        u_scales = keep.tile([P, POSITIONS, PIXELS], U8, align_bytes=64)
+        w_codes = keep.tile([P, POSITIONS, CH_OUT], U32, align_bytes=64)
+        w_scales = keep.tile([P, POSITIONS, CH_OUT], U8, align_bytes=64)
+
+        def spread(column):
+            spread_ps = ps_misc.tile([P, P], F32, tag="misc", name="spread_ps")
+            nc.tensor.transpose(spread_ps, column.to_broadcast([P, P]), ident)
+            return spread_ps
+
+        def inverse_scaled_norm(sum_sq, label):
+            z2 = small.tile([P, 1], F32, name="z2_" + label)
+            nc.vector.tensor_scalar(
+                out=z2, in0=sum_sq, scalar1=EPS * EPS, scalar2=SQRT_C * SQRT_C, op0=ALU.max, op1=ALU.mult
+            )
+            inv_z = small.tile([P, 1], F32, name="inv_z_" + label)
+            nc.gpsimd.tensor_tensor(out=inv_z, in0=z2, in1=neg_half, op=ALU.pow)
+            return z2, inv_z
+
+        grouped_tiles = {}
+
+        def flip_and_regroup(k):
+            words = w_rows[k].bitcast(F32)
+            flipped = ps_w.tile([P, HALVES * 2, P], F32, name="flipped")
+            for hu in range(HALVES * 2):
+                nc.tensor.transpose(flipped[:, hu, :], words[:, hu * P : (hu + 1) * P], ident)
+            grouped = w_stage.tile([P, HALVES, P, 2], F32, align_bytes=64, name="grouped")
+            nc.scalar.copy(out=grouped, in_=flipped.rearrange("q (h u) m -> q h m u", u=2))
+            grouped_tiles[k] = grouped
+
+        def quantise_weights(k):
+            nc.vector.quantize_mx(
+                out=w_codes[:, k, :].bitcast(FP8X4),
+                scales=w_scales[:, k, :],
+                in_=grouped_tiles[k].rearrange("q h m u -> q (h m u)").bitcast(BF16),
+            )
+
+
+        bias_f = small.tile([P, HALVES], F32)
+        nc.vector.tensor_copy(out=bias_f, in_=bias_bf)
+        bias_all = keep.tile([P, HALVES, P], F32)
+        for h in range(HALVES):
+            nc.vector.tensor_copy(out=bias_all[:, h, :], in_=spread(bias_f[:, h : h + 1]))
+
+        gram = ps_misc.tile([P, PIXELS], F32, tag="misc")
+        for t in range(PACK):
+            nc.tensor.matmul(
+                out=gram, lhsT=x_sb[:, t, :], rhs=x_sb[:, t, :], start=(t == 0), stop=(t == PACK - 1)
+            )
+        diagonal = keep.tile([P, PIXELS], F32)
+        norm_sq = small.tile([P, 1], F32)
+        nc.vector.scalar_tensor_tensor(
+            out=diagonal, in0=gram, scalar=1.0, in1=ident, op0=ALU.mult, op1=ALU.mult, accum_out=norm_sq
+        )
+        z2, inv_z = inverse_scaled_norm(norm_sq, "in")
+
+        flip_and_regroup(0)
+
+        z = small.tile([P, 1], F32)
+        nc.vector.tensor_scalar(
+            out=z, in0=z2, scalar1=inv_z, scalar2=1.0 - 1e-6, op0=ALU.mult, op1=ALU.min
+        )
+        half_inv_z = small.tile([P, 1], F32)
+        nc.vector.tensor_scalar_mul(out=half_inv_z, in0=inv_z, scalar1=0.5)
+        ln_plus = small.tile([P, 1], F32)
+        nc.scalar.activation(out=ln_plus, in_=z, func=ACT.Ln, bias=one, scale=1.0)
+        ln_minus = small.tile([P, 1], F32)
+        nc.scalar.activation(out=ln_minus, in_=z, func=ACT.Ln, bias=one, scale=-1.0)
+
+        flip_and_regroup(1)
+        quantise_weights(0)
+
+        factor = small.tile([P, 1], F32)
+        nc.vector.tensor_scalar(
+            out=factor, in0=ln_plus, scalar1=ln_minus, scalar2=half_inv_z, op0=ALU.subtract, op1=ALU.mult
+        )
+        flip_and_regroup(2)
+        factor_all = spread(factor)
+        middle = u_pad[:, PLANE + ROW_STEP : PLANE + ROW_STEP + PIXELS, :]
+        middle_by_batch = middle.rearrange("q (r b s) t -> q b r s t", r=ROWS, b=BATCH)
+        x_by_batch = x_sb.rearrange("q t (b r s) -> q b r s t", b=BATCH, r=ROWS)
+        for b in range(BATCH):
+            nc.vector.tensor_tensor(
+                out=middle_by_batch[:, b],
+                in0=x_by_batch[:, b],
+                in1=factor_all[:, b * IMAGE : (b + 1) * IMAGE]
+                .rearrange("q (r s) -> q r s", r=ROWS)
+                .unsqueeze(3)
+                .to_broadcast([P, ROWS, COLS, PACK]),
+                op=ALU.mult,
+            )
+        quantise_weights(1)
+
+        flip_and_regroup(3)
+        middle_rows = middle.rearrange("q (g s) t -> q g s t", s=COLS)
+        left = u_pad[:, ROW_STEP : ROW_STEP + PIXELS, :].rearrange("q (g s) t -> q g s t", s=COLS)
+        right_start = 2 * PLANE + ROW_STEP
+        right = u_pad[:, right_start : right_start + PIXELS, :].rearrange("q (g s) t -> q g s t", s=COLS)
+        nc.vector.tensor_copy(out=left[:, :, 1:COLS, :], in_=middle_rows[:, :, 0 : COLS - 1, :])
+        nc.vector.tensor_copy(out=right[:, :, 0 : COLS - 1, :], in_=middle_rows[:, :, 1:COLS, :])
+        quantise_weights(2)
+
+        flip_and_regroup(4)
+        nc.vector.quantize_mx(
+            out=u_codes.bitcast(FP8X4), scales=u_scales_raw, in_=u_pad.rearrange("q c t -> q (c t)")
+        )
+        quantise_weights(3)
+
+        flip_and_regroup(5)
+        raw_planes = u_scales_raw.bitcast(I32)[:, 0 : TAPS * PLANE // 4].rearrange("q (j c) -> q j c", j=TAPS)
+        for i in range(TAPS):
+            nc.vector.tensor_copy(
+                out=u_scales.bitcast(I32)[:, TAPS * i : TAPS * (i + 1), :],
+                in_=raw_planes[:, :, i * ROW_STEP // 4 : (i * ROW_STEP + PIXELS) // 4],
+            )
+        quantise_weights(4)
+
+        for k in range(6, POSITIONS):
+            flip_and_regroup(k)
+            quantise_weights(k - 1)
+        quantise_weights(POSITIONS - 1)
+
+        acc = ps_acc.tile([P, CH_OUT], F32)
+        for k in range(POSITIONS):
+            i, j = divmod(k, TAPS)
+            window = j * PLANE + i * ROW_STEP
+            nc.tensor.matmul_mx(
+                out=acc,
+                lhsT=u_codes[:, window : window + PIXELS].bitcast(FP8X4),
+                lhsT_scale=u_scales[:, k, :],
+                rhs=w_codes[:, k, :].bitcast(FP8X4),
+                rhs_scale=w_scales[:, k, :],
+                start=(k == 0),
+                stop=(k == POSITIONS - 1),
+            )
+
+        pre = keep.tile([P, HALVES, P], F32)
+        pre_flat = pre.rearrange("q h m -> q (h m)")
+        nc.vector.tensor_tensor(out=pre_flat, in0=acc, in1=bias_all.rearrange("q h m -> q (h m)"), op=ALU.add)
+        relu_sq = keep.tile([P, CH_OUT], F32)
+        sum_sq = small.tile([P, 1], F32)
+        nc.vector.scalar_tensor_tensor(
+            out=relu_sq, in0=pre_flat, scalar=0.0, in1=pre_flat, op0=ALU.max, op1=ALU.mult, accum_out=sum_sq
+        )
+        y2, inv_y = inverse_scaled_norm(sum_sq, "out")
+        tanh_y = small.tile([P, 1], F32)
+        nc.scalar.activation(out=tanh_y, in_=y2, func=ACT.Tanh, scale=inv_y)
+        gain = small.tile([P, 1], F32)
+        nc.vector.tensor_mul(out=gain, in0=tanh_y, in1=inv_y)
+        scaled = keep.tile([P, HALVES, P], F32)
+        nc.vector.tensor_scalar(
+            out=scaled[:, 0, :], in0=pre[:, 0, :], scalar1=0.0, scalar2=gain, op0=ALU.max, op1=ALU.mult
+        )
+        nc.scalar.activation(out=scaled[:, 1, :], in_=pre[:, 1, :], func=ACT.Relu, scale=gain)
+
+        out_sb = keep.tile([P, BATCH, HALVES, IMAGE], F32)
+        for h in range(HALVES):
+            back = ps_misc.tile([P, PIXELS], F32, tag="misc")
+            nc.tensor.transpose(back, scaled[:, h, :], ident)
+            src = back.rearrange("m (r b s) -> m b r s", r=ROWS, b=BATCH)
+            dst = out_sb[:, :, h, :].rearrange("m b (r s) -> m b r s", r=ROWS)
+            if h == 0:
+                nc.vector.tensor_copy(out=dst, in_=src)
+            else:
+                nc.scalar.copy(out=dst, in_=src)
+        nc.sync.dma_start(
+            out=out.rearrange("b (m h) r s -> m b (h r s)", h=HALVES),
+            in_=out_sb.rearrange("m b h p -> m b (h p)"),
+        )

@@ -18,10 +18,13 @@ IMAGE = ROWS * COLS
 PIXELS = BATCH * IMAGE
 PACK = 4
 HALVES = CH_OUT // P
+BOTH = range(HALVES)
 
 ROW_STEP = BATCH * COLS
 PLANE = (ROWS + 2) * ROW_STEP
-PAD_COLS = 512
+SCALE_PAD = 64
+SCALE_PLANE = PIXELS + 2 * SCALE_PAD
+WARM_UPS = 3
 
 SQRT_C = 0.1
 EPS = 1e-7
@@ -34,23 +37,28 @@ def tile_pvconv2d_s_kernel(tc, x, Wk, bias, out):
         tc.tile_pool(name="keep", bufs=1) as keep,
         tc.tile_pool(name="small", bufs=1) as small,
         tc.tile_pool(name="w_in", bufs=POSITIONS) as w_in,
-        tc.tile_pool(name="w_stage", bufs=3) as w_stage,
+        tc.tile_pool(name="w_stage", bufs=POSITIONS) as w_stage,
         tc.psum_pool(name="ps_w", bufs=4) as ps_w,
         tc.psum_pool(name="ps_acc", bufs=1) as ps_acc,
         tc.psum_pool(name="ps_misc", bufs=3) as ps_misc,
         tc.manual_schedule(),
     ):
+        w_rows = []
+
+        def load_weights(k):
+            rows = w_in.tile([P, HALVES * CH_IN], BF16, name="w_rows")
+            nc.sync.dma_start(out=rows, in_=Wk[k].rearrange("(m h) c -> m (h c)", h=HALVES))
+            w_rows.append(rows)
+
+        load_weights(0)
         x_sb = keep.tile([P, PACK, PIXELS], BF16)
         x_by_t = x.rearrange("b (u q e) r s -> u e q b (r s)", u=2, q=P, e=2)
         for t in range(PACK):
             nc.sync.dma_start(
                 out=x_sb[:, t, :].rearrange("q (b p) -> q b p", b=BATCH), in_=x_by_t[t // 2, t % 2]
             )
-        w_rows = []
-        for k in range(POSITIONS):
-            rows = w_in.tile([P, HALVES * CH_IN], BF16, name="w_rows")
-            nc.sync.dma_start(out=rows, in_=Wk[k].rearrange("(m h) c -> m (h c)", h=HALVES))
-            w_rows.append(rows)
+        for k in range(1, POSITIONS):
+            load_weights(k)
         bias_bf = small.tile([P, HALVES], BF16)
         nc.scalar.dma_start(out=bias_bf, in_=bias.rearrange("(m h) -> m h", h=HALVES))
 
@@ -62,40 +70,58 @@ def tile_pvconv2d_s_kernel(tc, x, Wk, bias, out):
         nc.scalar.activation(out=warm, in_=one, func=ACT.Ln)
         ident = keep.tile([P, P], F32)
         make_identity(nc, ident)
+        ident_4c = keep.tile([P, P], F32)
+        nc.gpsimd.tensor_scalar_mul(out=ident_4c, in0=ident, scalar1=4 * SQRT_C * SQRT_C)
+        ident_brs = keep.tile([P, PIXELS], F32)
+        nc.gpsimd.tensor_copy(
+            out=ident_brs.rearrange("p (b r s) -> p b r s", b=BATCH, r=ROWS),
+            in_=ident.rearrange("p (r b s) -> p b r s", r=ROWS, b=BATCH),
+        )
+        unread = ps_misc.tile([P, P], F32, tag="misc")
+        for n in range(WARM_UPS):
+            nc.tensor.matmul(out=unread, lhsT=ident, rhs=ident, start=True, stop=True)
 
-        u_pad = keep.tile([P, PAD_COLS, PACK], BF16, align_bytes=64)
-        nc.vector.memset(u_pad, 0.0)
-        u_codes = keep.tile([P, PAD_COLS], U32, align_bytes=64)
-        u_scales_raw = keep.tile([P, PAD_COLS], U8, align_bytes=64)
-        nc.vector.memset(u_scales_raw.bitcast(I32), 0)
-        u_scales = keep.tile([P, POSITIONS, PIXELS], U8, align_bytes=64)
+        u_codes = keep.tile([P, TAPS, PLANE], U32, align_bytes=64)
+        nc.vector.memset(u_codes.bitcast(I32), 0)
+        u_scales = keep.tile([P, TAPS, SCALE_PLANE], U8, align_bytes=64)
+        nc.vector.memset(u_scales.bitcast(I32), 0)
+        u_scales_up = keep.tile([P, TAPS, PIXELS], U8, align_bytes=64)
+        u_scales_down = keep.tile([P, TAPS, PIXELS], U8, align_bytes=64)
         w_codes = keep.tile([P, POSITIONS, CH_OUT], U32, align_bytes=64)
         w_scales = keep.tile([P, POSITIONS, CH_OUT], U8, align_bytes=64)
 
-        def spread(column):
+        def spread(column, order):
             spread_ps = ps_misc.tile([P, P], F32, tag="misc", name="spread_ps")
-            nc.tensor.transpose(spread_ps, column.to_broadcast([P, P]), ident)
+            nc.tensor.transpose(spread_ps, column.to_broadcast([P, P]), order)
             return spread_ps
 
-        def inverse_scaled_norm(sum_sq, label):
-            z2 = small.tile([P, 1], F32, name="z2_" + label)
-            nc.vector.tensor_scalar(
-                out=z2, in0=sum_sq, scalar1=EPS * EPS, scalar2=SQRT_C * SQRT_C, op0=ALU.max, op1=ALU.mult
-            )
-            inv_z = small.tile([P, 1], F32, name="inv_z_" + label)
-            nc.gpsimd.tensor_tensor(out=inv_z, in0=z2, in1=neg_half, op=ALU.pow)
-            return z2, inv_z
+        def inverse_root(column, name):
+            inverse = small.tile([P, 1], F32, name=name)
+            nc.gpsimd.tensor_tensor(out=inverse, in0=column, in1=neg_half, op=ALU.pow)
+            return inverse
 
         grouped_tiles = {}
 
-        def flip_and_regroup(k):
+        def flip(k, halves):
             words = w_rows[k].bitcast(F32)
             flipped = ps_w.tile([P, HALVES * 2, P], F32, name="flipped")
-            for hu in range(HALVES * 2):
-                nc.tensor.transpose(flipped[:, hu, :], words[:, hu * P : (hu + 1) * P], ident)
-            grouped = w_stage.tile([P, HALVES, P, 2], F32, align_bytes=64, name="grouped")
-            nc.scalar.copy(out=grouped, in_=flipped.rearrange("q (h u) m -> q h m u", u=2))
-            grouped_tiles[k] = grouped
+            for h in halves:
+                for u in range(2):
+                    hu = 2 * h + u
+                    nc.tensor.transpose(flipped[:, hu, :], words[:, hu * P : (hu + 1) * P], ident)
+            return flipped
+
+        def regroup(k, flipped, halves, copy):
+            if k not in grouped_tiles:
+                grouped_tiles[k] = w_stage.tile([P, HALVES, P, 2], F32, align_bytes=64, name="grouped")
+            lo, hi = halves[0], halves[-1] + 1
+            copy(
+                out=grouped_tiles[k][:, lo:hi],
+                in_=flipped[:, 2 * lo : 2 * hi].rearrange("q (h u) m -> q h m u", u=2),
+            )
+
+        def flip_and_regroup(k, copy=nc.scalar.copy):
+            regroup(k, flip(k, BOTH), BOTH, copy)
 
         def quantise_weights(k):
             nc.vector.quantize_mx(
@@ -104,12 +130,12 @@ def tile_pvconv2d_s_kernel(tc, x, Wk, bias, out):
                 in_=grouped_tiles[k].rearrange("q h m u -> q (h m u)").bitcast(BF16),
             )
 
-
+        pre = keep.tile([P, CH_OUT + 1], F32)
+        nc.gpsimd.tensor_scalar_mul(out=pre[:, CH_OUT:], in0=one, scalar1=SQRT_C * EPS)
         bias_f = small.tile([P, HALVES], F32)
-        nc.vector.tensor_copy(out=bias_f, in_=bias_bf)
-        bias_all = keep.tile([P, HALVES, P], F32)
-        for h in range(HALVES):
-            nc.vector.tensor_copy(out=bias_all[:, h, :], in_=spread(bias_f[:, h : h + 1]))
+        nc.gpsimd.tensor_scalar_mul(out=bias_f, in0=bias_bf, scalar1=SQRT_C)
+
+        flip_and_regroup(0)
 
         gram = ps_misc.tile([P, PIXELS], F32, tag="misc")
         for t in range(PACK):
@@ -117,40 +143,41 @@ def tile_pvconv2d_s_kernel(tc, x, Wk, bias, out):
                 out=gram, lhsT=x_sb[:, t, :], rhs=x_sb[:, t, :], start=(t == 0), stop=(t == PACK - 1)
             )
         diagonal = keep.tile([P, PIXELS], F32)
-        norm_sq = small.tile([P, 1], F32)
+        twice_z_sq = small.tile([P, 1], F32)
         nc.vector.scalar_tensor_tensor(
-            out=diagonal, in0=gram, scalar=1.0, in1=ident, op0=ALU.mult, op1=ALU.mult, accum_out=norm_sq
+            out=diagonal, in0=gram, scalar=EPS * EPS, in1=ident_4c, op0=ALU.add, op1=ALU.mult, accum_out=twice_z_sq
         )
-        z2, inv_z = inverse_scaled_norm(norm_sq, "in")
-
-        flip_and_regroup(0)
-
-        z = small.tile([P, 1], F32)
-        nc.vector.tensor_scalar(
-            out=z, in0=z2, scalar1=inv_z, scalar2=1.0 - 1e-6, op0=ALU.mult, op1=ALU.min
+        half_inv_z = inverse_root(twice_z_sq, "half_inv_z")
+        twice_z = small.tile([P, 1], F32)
+        nc.gpsimd.tensor_scalar(
+            out=twice_z, in0=twice_z_sq, scalar1=half_inv_z, scalar2=2 * (1.0 - 1e-6), op0=ALU.mult, op1=ALU.min
         )
-        half_inv_z = small.tile([P, 1], F32)
-        nc.vector.tensor_scalar_mul(out=half_inv_z, in0=inv_z, scalar1=0.5)
-        ln_plus = small.tile([P, 1], F32)
-        nc.scalar.activation(out=ln_plus, in_=z, func=ACT.Ln, bias=one, scale=1.0)
-        ln_minus = small.tile([P, 1], F32)
-        nc.scalar.activation(out=ln_minus, in_=z, func=ACT.Ln, bias=one, scale=-1.0)
-
-        flip_and_regroup(1)
         quantise_weights(0)
+        flip_and_regroup(1, nc.vector.tensor_copy)
+        quantise_weights(1)
+        flip_and_regroup(2)
+
+        ln_plus = small.tile([P, 1], F32)
+        nc.scalar.activation(out=ln_plus, in_=twice_z, func=ACT.Ln, bias=one, scale=0.5)
+        ln_minus = small.tile([P, 1], F32)
+        nc.scalar.activation(out=ln_minus, in_=twice_z, func=ACT.Ln, bias=one, scale=-0.5)
+        quantise_weights(2)
 
         factor = small.tile([P, 1], F32)
-        nc.vector.tensor_scalar(
+        nc.gpsimd.tensor_scalar(
             out=factor, in0=ln_plus, scalar1=ln_minus, scalar2=half_inv_z, op0=ALU.subtract, op1=ALU.mult
         )
-        flip_and_regroup(2)
-        factor_all = spread(factor)
-        middle = u_pad[:, PLANE + ROW_STEP : PLANE + ROW_STEP + PIXELS, :]
-        middle_by_batch = middle.rearrange("q (r b s) t -> q b r s t", r=ROWS, b=BATCH)
+        flip_and_regroup(3)
+        quantise_weights(3)
+        flip_and_regroup(4)
+        flip_and_regroup(5)
+        factor_all = spread(factor, ident)
+        u_bf = keep.tile([P, PIXELS, PACK], BF16, align_bytes=64)
+        u_by_batch = u_bf.rearrange("q (r b s) t -> q b r s t", r=ROWS, b=BATCH)
         x_by_batch = x_sb.rearrange("q t (b r s) -> q b r s t", b=BATCH, r=ROWS)
         for b in range(BATCH):
             nc.vector.tensor_tensor(
-                out=middle_by_batch[:, b],
+                out=u_by_batch[:, b],
                 in0=x_by_batch[:, b],
                 in1=factor_all[:, b * IMAGE : (b + 1) * IMAGE]
                 .rearrange("q (r s) -> q r s", r=ROWS)
@@ -158,80 +185,80 @@ def tile_pvconv2d_s_kernel(tc, x, Wk, bias, out):
                 .to_broadcast([P, ROWS, COLS, PACK]),
                 op=ALU.mult,
             )
-        quantise_weights(1)
-
-        flip_and_regroup(3)
-        middle_rows = middle.rearrange("q (g s) t -> q g s t", s=COLS)
-        left = u_pad[:, ROW_STEP : ROW_STEP + PIXELS, :].rearrange("q (g s) t -> q g s t", s=COLS)
-        right_start = 2 * PLANE + ROW_STEP
-        right = u_pad[:, right_start : right_start + PIXELS, :].rearrange("q (g s) t -> q g s t", s=COLS)
-        nc.vector.tensor_copy(out=left[:, :, 1:COLS, :], in_=middle_rows[:, :, 0 : COLS - 1, :])
-        nc.vector.tensor_copy(out=right[:, :, 0 : COLS - 1, :], in_=middle_rows[:, :, 1:COLS, :])
-        quantise_weights(2)
-
-        flip_and_regroup(4)
+        middle = 1
         nc.vector.quantize_mx(
-            out=u_codes.bitcast(FP8X4), scales=u_scales_raw, in_=u_pad.rearrange("q c t -> q (c t)")
+            out=u_codes[:, middle, ROW_STEP : ROW_STEP + PIXELS].bitcast(FP8X4),
+            scales=u_scales[:, middle, SCALE_PAD : SCALE_PAD + PIXELS],
+            in_=u_bf.rearrange("q n t -> q (n t)"),
         )
-        quantise_weights(3)
-
-        flip_and_regroup(5)
-        raw_planes = u_scales_raw.bitcast(I32)[:, 0 : TAPS * PLANE // 4].rearrange("q (j c) -> q j c", j=TAPS)
-        for i in range(TAPS):
-            nc.vector.tensor_copy(
-                out=u_scales.bitcast(I32)[:, TAPS * i : TAPS * (i + 1), :],
-                in_=raw_planes[:, :, i * ROW_STEP // 4 : (i * ROW_STEP + PIXELS) // 4],
-            )
         quantise_weights(4)
+        code_rows = u_codes[:, :, ROW_STEP : ROW_STEP + PIXELS].bitcast(I32).rearrange("q j (g s) -> q j g s", s=COLS)
+        scale_rows = u_scales[:, :, SCALE_PAD : SCALE_PAD + PIXELS].rearrange("q j (g s) -> q j g s", s=COLS)
+        for rows in (code_rows, scale_rows):
+            nc.vector.tensor_copy(out=rows[:, 0, :, 1:COLS], in_=rows[:, middle, :, 0 : COLS - 1])
+            nc.vector.tensor_copy(out=rows[:, 2, :, 0 : COLS - 1], in_=rows[:, middle, :, 1:COLS])
+        words = u_scales.bitcast(I32)
+        for moved, first in ((u_scales_up, SCALE_PAD - ROW_STEP), (u_scales_down, SCALE_PAD + ROW_STEP)):
+            nc.vector.tensor_copy(out=moved.bitcast(I32), in_=words[:, :, first // 4 : (first + PIXELS) // 4])
+        window_scales = (u_scales_up, u_scales[:, :, SCALE_PAD : SCALE_PAD + PIXELS], u_scales_down)
 
-        for k in range(6, POSITIONS):
+        for k in range(6, POSITIONS - 1):
             flip_and_regroup(k)
             quantise_weights(k - 1)
-        quantise_weights(POSITIONS - 1)
+        last = POSITIONS - 1
+        flipped_0 = flip(last, [0])
+        flipped_1 = flip(last, [1])
+        regroup(last, flipped_0, [0], nc.scalar.copy)
+        quantise_weights(last - 1)
+        regroup(last, flipped_1, [1], nc.vector.tensor_copy)
+        quantise_weights(last)
+
+        bias_ps = ps_misc.tile([P, HALVES, P], F32, tag="misc")
+        for h in BOTH:
+            nc.tensor.transpose(bias_ps[:, h, :], bias_f[:, h : h + 1].to_broadcast([P, P]), ident)
+        bias_all = keep.tile([P, HALVES, P], F32)
+        nc.scalar.copy(out=bias_all, in_=bias_ps)
+        nc.scalar.activation(out=warm, in_=one, func=ACT.Tanh)
 
         acc = ps_acc.tile([P, CH_OUT], F32)
         for k in range(POSITIONS):
             i, j = divmod(k, TAPS)
-            window = j * PLANE + i * ROW_STEP
             nc.tensor.matmul_mx(
                 out=acc,
-                lhsT=u_codes[:, window : window + PIXELS].bitcast(FP8X4),
-                lhsT_scale=u_scales[:, k, :],
+                lhsT=u_codes[:, j, i * ROW_STEP : i * ROW_STEP + PIXELS].bitcast(FP8X4),
+                lhsT_scale=window_scales[i][:, j, :],
                 rhs=w_codes[:, k, :].bitcast(FP8X4),
                 rhs_scale=w_scales[:, k, :],
                 start=(k == 0),
                 stop=(k == POSITIONS - 1),
             )
 
-        pre = keep.tile([P, HALVES, P], F32)
-        pre_flat = pre.rearrange("q h m -> q (h m)")
-        nc.vector.tensor_tensor(out=pre_flat, in0=acc, in1=bias_all.rearrange("q h m -> q (h m)"), op=ALU.add)
-        relu_sq = keep.tile([P, CH_OUT], F32)
-        sum_sq = small.tile([P, 1], F32)
         nc.vector.scalar_tensor_tensor(
-            out=relu_sq, in0=pre_flat, scalar=0.0, in1=pre_flat, op0=ALU.max, op1=ALU.mult, accum_out=sum_sq
+            out=pre[:, 0:CH_OUT], in0=acc, scalar=SQRT_C, in1=bias_all.rearrange("q h m -> q (h m)"), op0=ALU.mult, op1=ALU.add
         )
-        y2, inv_y = inverse_scaled_norm(sum_sq, "out")
+        back = ps_misc.tile([P, HALVES, PIXELS], F32, tag="misc")
+        for h in BOTH:
+            nc.tensor.transpose(back[:, h, :], pre[:, h * P : (h + 1) * P], ident_brs)
+        relu = keep.tile([P, HALVES, PIXELS], F32)
+        nc.scalar.activation(out=relu, in_=back, func=ACT.Relu, scale=1.0 / SQRT_C)
+        relu_sq = keep.tile([P, CH_OUT + 1], F32)
+        y_sq = small.tile([P, 1], F32)
+        nc.vector.scalar_tensor_tensor(
+            out=relu_sq, in0=pre, scalar=0.0, in1=pre, op0=ALU.max, op1=ALU.mult, accum_out=y_sq
+        )
+        inv_y = inverse_root(y_sq, "inv_y")
         tanh_y = small.tile([P, 1], F32)
-        nc.scalar.activation(out=tanh_y, in_=y2, func=ACT.Tanh, scale=inv_y)
+        nc.scalar.activation(out=tanh_y, in_=y_sq, func=ACT.Tanh, scale=inv_y)
         gain = small.tile([P, 1], F32)
-        nc.vector.tensor_mul(out=gain, in0=tanh_y, in1=inv_y)
-        scaled = keep.tile([P, HALVES, P], F32)
-        nc.vector.tensor_scalar(
-            out=scaled[:, 0, :], in0=pre[:, 0, :], scalar1=0.0, scalar2=gain, op0=ALU.max, op1=ALU.mult
-        )
-        nc.scalar.activation(out=scaled[:, 1, :], in_=pre[:, 1, :], func=ACT.Relu, scale=gain)
-
+        nc.scalar.activation(out=gain, in_=tanh_y, func=ACT.Copy, scale=inv_y)
+        gain_all = spread(gain, ident_brs)
         out_sb = keep.tile([P, BATCH, HALVES, IMAGE], F32)
-        for h in range(HALVES):
-            back = ps_misc.tile([P, PIXELS], F32, tag="misc")
-            nc.tensor.transpose(back, scaled[:, h, :], ident)
-            src = back.rearrange("m (r b s) -> m b r s", r=ROWS, b=BATCH)
-            dst = out_sb[:, :, h, :].rearrange("m b (r s) -> m b r s", r=ROWS)
-            if h == 0:
-                nc.vector.tensor_copy(out=dst, in_=src)
-            else:
-                nc.scalar.copy(out=dst, in_=src)
+        nc.vector.tensor_tensor(
+            out=out_sb,
+            in0=relu.rearrange("m h (b p) -> m b h p", b=BATCH),
+            in1=gain_all.rearrange("m (b p) -> m b p", b=BATCH).unsqueeze(2).to_broadcast([P, BATCH, HALVES, IMAGE]),
+            op=ALU.mult,
+        )
         nc.sync.dma_start(
             out=out.rearrange("b (m h) r s -> m b (h r s)", h=HALVES),
             in_=out_sb.rearrange("m b h p -> m b (h p)"),

@@ -70,13 +70,6 @@ def tile_pvconv2d_s_kernel(tc, x, Wk, bias, out):
         nc.scalar.activation(out=warm, in_=one, func=ACT.Ln)
         ident = keep.tile([P, P], F32)
         make_identity(nc, ident)
-        ident_4c = keep.tile([P, P], F32)
-        nc.gpsimd.tensor_scalar_mul(out=ident_4c, in0=ident, scalar1=4 * SQRT_C * SQRT_C)
-        ident_brs = keep.tile([P, PIXELS], F32)
-        nc.gpsimd.tensor_copy(
-            out=ident_brs.rearrange("p (b r s) -> p b r s", b=BATCH, r=ROWS),
-            in_=ident.rearrange("p (r b s) -> p b r s", r=ROWS, b=BATCH),
-        )
         unread = ps_misc.tile([P, P], F32, tag="misc")
         for n in range(WARM_UPS):
             nc.tensor.matmul(out=unread, lhsT=ident, rhs=ident, start=True, stop=True)
@@ -85,6 +78,13 @@ def tile_pvconv2d_s_kernel(tc, x, Wk, bias, out):
         nc.vector.memset(u_codes.bitcast(I32), 0)
         u_scales = keep.tile([P, TAPS, SCALE_PLANE], U8, align_bytes=64)
         nc.vector.memset(u_scales.bitcast(I32), 0)
+        ident_4c = keep.tile([P, P], F32)
+        nc.vector.tensor_scalar_mul(out=ident_4c, in0=ident, scalar1=4 * SQRT_C * SQRT_C)
+        ident_brs = keep.tile([P, PIXELS], F32)
+        nc.vector.tensor_copy(
+            out=ident_brs.rearrange("p (b r s) -> p b r s", b=BATCH, r=ROWS),
+            in_=ident.rearrange("p (r b s) -> p b r s", r=ROWS, b=BATCH),
+        )
         u_scales_up = keep.tile([P, TAPS, PIXELS], U8, align_bytes=64)
         u_scales_down = keep.tile([P, TAPS, PIXELS], U8, align_bytes=64)
         w_codes = keep.tile([P, POSITIONS, CH_OUT], U32, align_bytes=64)
@@ -102,26 +102,14 @@ def tile_pvconv2d_s_kernel(tc, x, Wk, bias, out):
 
         grouped_tiles = {}
 
-        def flip(k, halves):
+        def flip_and_regroup(k, copy=nc.scalar.copy):
             words = w_rows[k].bitcast(F32)
             flipped = ps_w.tile([P, HALVES * 2, P], F32, name="flipped")
-            for h in halves:
-                for u in range(2):
-                    hu = 2 * h + u
-                    nc.tensor.transpose(flipped[:, hu, :], words[:, hu * P : (hu + 1) * P], ident)
-            return flipped
-
-        def regroup(k, flipped, halves, copy):
-            if k not in grouped_tiles:
-                grouped_tiles[k] = w_stage.tile([P, HALVES, P, 2], F32, align_bytes=64, name="grouped")
-            lo, hi = halves[0], halves[-1] + 1
-            copy(
-                out=grouped_tiles[k][:, lo:hi],
-                in_=flipped[:, 2 * lo : 2 * hi].rearrange("q (h u) m -> q h m u", u=2),
-            )
-
-        def flip_and_regroup(k, copy=nc.scalar.copy):
-            regroup(k, flip(k, BOTH), BOTH, copy)
+            for hu in range(HALVES * 2):
+                nc.tensor.transpose(flipped[:, hu, :], words[:, hu * P : (hu + 1) * P], ident)
+            grouped = w_stage.tile([P, HALVES, P, 2], F32, align_bytes=64, name="grouped")
+            copy(out=grouped, in_=flipped.rearrange("q (h u) m -> q h m u", u=2))
+            grouped_tiles[k] = grouped
 
         def quantise_weights(k):
             nc.vector.quantize_mx(
@@ -131,9 +119,9 @@ def tile_pvconv2d_s_kernel(tc, x, Wk, bias, out):
             )
 
         pre = keep.tile([P, CH_OUT + 1], F32)
-        nc.gpsimd.tensor_scalar_mul(out=pre[:, CH_OUT:], in0=one, scalar1=SQRT_C * EPS)
+        nc.vector.tensor_scalar_mul(out=pre[:, CH_OUT:], in0=one, scalar1=SQRT_C * EPS)
         bias_f = small.tile([P, HALVES], F32)
-        nc.gpsimd.tensor_scalar_mul(out=bias_f, in0=bias_bf, scalar1=SQRT_C)
+        nc.scalar.activation(out=bias_f, in_=bias_bf, func=ACT.Copy, scale=SQRT_C)
 
         flip_and_regroup(0)
 
@@ -148,30 +136,28 @@ def tile_pvconv2d_s_kernel(tc, x, Wk, bias, out):
             out=diagonal, in0=gram, scalar=EPS * EPS, in1=ident_4c, op0=ALU.add, op1=ALU.mult, accum_out=twice_z_sq
         )
         half_inv_z = inverse_root(twice_z_sq, "half_inv_z")
+        flip_and_regroup(1, nc.vector.tensor_copy)
+        flip_and_regroup(2)
+
         twice_z = small.tile([P, 1], F32)
-        nc.gpsimd.tensor_scalar(
+        nc.vector.tensor_scalar(
             out=twice_z, in0=twice_z_sq, scalar1=half_inv_z, scalar2=2 * (1.0 - 1e-6), op0=ALU.mult, op1=ALU.min
         )
         quantise_weights(0)
-        flip_and_regroup(1, nc.vector.tensor_copy)
-        quantise_weights(1)
-        flip_and_regroup(2)
-
         ln_plus = small.tile([P, 1], F32)
         nc.scalar.activation(out=ln_plus, in_=twice_z, func=ACT.Ln, bias=one, scale=0.5)
         ln_minus = small.tile([P, 1], F32)
         nc.scalar.activation(out=ln_minus, in_=twice_z, func=ACT.Ln, bias=one, scale=-0.5)
-        quantise_weights(2)
-
         factor = small.tile([P, 1], F32)
-        nc.gpsimd.tensor_scalar(
+        nc.vector.tensor_scalar(
             out=factor, in0=ln_plus, scalar1=ln_minus, scalar2=half_inv_z, op0=ALU.subtract, op1=ALU.mult
         )
+        quantise_weights(1)
         flip_and_regroup(3)
-        quantise_weights(3)
         flip_and_regroup(4)
-        flip_and_regroup(5)
         factor_all = spread(factor, ident)
+        flip_and_regroup(5)
+        quantise_weights(2)
         u_bf = keep.tile([P, PIXELS, PACK], BF16, align_bytes=64)
         u_by_batch = u_bf.rearrange("q (r b s) t -> q b r s t", r=ROWS, b=BATCH)
         x_by_batch = x_sb.rearrange("q t (b r s) -> q b r s t", b=BATCH, r=ROWS)
@@ -191,7 +177,6 @@ def tile_pvconv2d_s_kernel(tc, x, Wk, bias, out):
             scales=u_scales[:, middle, SCALE_PAD : SCALE_PAD + PIXELS],
             in_=u_bf.rearrange("q n t -> q (n t)"),
         )
-        quantise_weights(4)
         code_rows = u_codes[:, :, ROW_STEP : ROW_STEP + PIXELS].bitcast(I32).rearrange("q j (g s) -> q j g s", s=COLS)
         scale_rows = u_scales[:, :, SCALE_PAD : SCALE_PAD + PIXELS].rearrange("q j (g s) -> q j g s", s=COLS)
         for rows in (code_rows, scale_rows):
@@ -202,16 +187,10 @@ def tile_pvconv2d_s_kernel(tc, x, Wk, bias, out):
             nc.vector.tensor_copy(out=moved.bitcast(I32), in_=words[:, :, first // 4 : (first + PIXELS) // 4])
         window_scales = (u_scales_up, u_scales[:, :, SCALE_PAD : SCALE_PAD + PIXELS], u_scales_down)
 
-        for k in range(6, POSITIONS - 1):
+        for k in range(6, POSITIONS):
             flip_and_regroup(k)
-            quantise_weights(k - 1)
-        last = POSITIONS - 1
-        flipped_0 = flip(last, [0])
-        flipped_1 = flip(last, [1])
-        regroup(last, flipped_0, [0], nc.scalar.copy)
-        quantise_weights(last - 1)
-        regroup(last, flipped_1, [1], nc.vector.tensor_copy)
-        quantise_weights(last)
+        for k in range(3, POSITIONS):
+            quantise_weights(k)
 
         bias_ps = ps_misc.tile([P, HALVES, P], F32, tag="misc")
         for h in BOTH:

@@ -157,7 +157,6 @@ def tile_pvconv2d_s_kernel(tc, x, Wk, bias, out):
         flip_and_regroup(4)
         factor_all = spread(factor, ident)
         flip_and_regroup(5)
-        quantise_weights(2)
         u_bf = keep.tile([P, PIXELS, PACK], BF16, align_bytes=64)
         u_by_batch = u_bf.rearrange("q (r b s) t -> q b r s t", r=ROWS, b=BATCH)
         x_by_batch = x_sb.rearrange("q t (b r s) -> q b r s t", b=BATCH, r=ROWS)
@@ -171,25 +170,28 @@ def tile_pvconv2d_s_kernel(tc, x, Wk, bias, out):
                 .to_broadcast([P, ROWS, COLS, PACK]),
                 op=ALU.mult,
             )
+        for k in range(6, POSITIONS):
+            flip_and_regroup(k)
+
+        quantise_weights(2)
         middle = 1
         nc.vector.quantize_mx(
             out=u_codes[:, middle, ROW_STEP : ROW_STEP + PIXELS].bitcast(FP8X4),
             scales=u_scales[:, middle, SCALE_PAD : SCALE_PAD + PIXELS],
             in_=u_bf.rearrange("q n t -> q (n t)"),
         )
+        quantise_weights(3)
         code_rows = u_codes[:, :, ROW_STEP : ROW_STEP + PIXELS].bitcast(I32).rearrange("q j (g s) -> q j g s", s=COLS)
         scale_rows = u_scales[:, :, SCALE_PAD : SCALE_PAD + PIXELS].rearrange("q j (g s) -> q j g s", s=COLS)
-        for rows in (code_rows, scale_rows):
+        for rows in (scale_rows, code_rows):
             nc.vector.tensor_copy(out=rows[:, 0, :, 1:COLS], in_=rows[:, middle, :, 0 : COLS - 1])
             nc.vector.tensor_copy(out=rows[:, 2, :, 0 : COLS - 1], in_=rows[:, middle, :, 1:COLS])
+        quantise_weights(4)
         words = u_scales.bitcast(I32)
         for moved, first in ((u_scales_up, SCALE_PAD - ROW_STEP), (u_scales_down, SCALE_PAD + ROW_STEP)):
             nc.vector.tensor_copy(out=moved.bitcast(I32), in_=words[:, :, first // 4 : (first + PIXELS) // 4])
         window_scales = (u_scales_up, u_scales[:, :, SCALE_PAD : SCALE_PAD + PIXELS], u_scales_down)
-
-        for k in range(6, POSITIONS):
-            flip_and_regroup(k)
-        for k in range(3, POSITIONS):
+        for k in range(5, POSITIONS):
             quantise_weights(k)
 
         bias_ps = ps_misc.tile([P, HALVES, P], F32, tag="misc")

@@ -24,7 +24,7 @@ ROW_STEP = BATCH * COLS
 PLANE = (ROWS + 2) * ROW_STEP
 SCALE_PAD = 64
 SCALE_PLANE = PIXELS + 2 * SCALE_PAD
-WARM_UPS = 3
+MX_WARM_UPS = 12
 
 SQRT_C = 0.1
 EPS = 1e-7
@@ -70,8 +70,26 @@ def tile_pvconv2d_s_kernel(tc, x, Wk, bias, out):
         nc.scalar.activation(out=warm, in_=one, func=ACT.Ln)
         ident = keep.tile([P, P], F32)
         make_identity(nc, ident)
+
+        zeros = keep.tile([P, PIXELS * PACK], BF16, align_bytes=64)
+        nc.vector.memset(zeros.bitcast(I32), 0)
+        zero_codes = keep.tile([P, PIXELS], U32, align_bytes=64)
+        zero_scales = keep.tile([P, PIXELS], U8, align_bytes=64)
+        nc.vector.quantize_mx(out=zero_codes.bitcast(FP8X4), scales=zero_scales, in_=zeros)
         unread = ps_misc.tile([P, P], F32, tag="misc")
-        for n in range(WARM_UPS):
+        for n in range(MX_WARM_UPS):
+            nc.tensor.matmul_mx(
+                out=unread,
+                lhsT=zero_codes.bitcast(FP8X4),
+                lhsT_scale=zero_scales,
+                rhs=zero_codes.bitcast(FP8X4),
+                rhs_scale=zero_scales,
+                start=True,
+                stop=True,
+            )
+
+        def keep_warm():
+            unread = ps_misc.tile([P, P], F32, tag="misc")
             nc.tensor.matmul(out=unread, lhsT=ident, rhs=ident, start=True, stop=True)
 
         u_codes = keep.tile([P, TAPS, PLANE], U32, align_bytes=64)
@@ -138,6 +156,7 @@ def tile_pvconv2d_s_kernel(tc, x, Wk, bias, out):
         half_inv_z = inverse_root(twice_z_sq, "half_inv_z")
         flip_and_regroup(1, nc.vector.tensor_copy)
         flip_and_regroup(2)
+        keep_warm()
 
         twice_z = small.tile([P, 1], F32)
         nc.vector.tensor_scalar(
@@ -155,6 +174,7 @@ def tile_pvconv2d_s_kernel(tc, x, Wk, bias, out):
         quantise_weights(1)
         flip_and_regroup(3)
         flip_and_regroup(4)
+        keep_warm()
         factor_all = spread(factor, ident)
         flip_and_regroup(5)
         u_bf = keep.tile([P, PIXELS, PACK], BF16, align_bytes=64)
@@ -170,6 +190,7 @@ def tile_pvconv2d_s_kernel(tc, x, Wk, bias, out):
                 .to_broadcast([P, ROWS, COLS, PACK]),
                 op=ALU.mult,
             )
+        keep_warm()
         for k in range(6, POSITIONS):
             flip_and_regroup(k)
 

@@ -24,7 +24,7 @@ ROW_STEP = BATCH * COLS
 PLANE = (ROWS + 2) * ROW_STEP
 SCALE_PAD = 64
 SCALE_PLANE = PIXELS + 2 * SCALE_PAD
-MX_WARM_UPS = 12
+MX_WARM_UPS = 10
 
 SQRT_C = 0.1
 EPS = 1e-7
@@ -60,16 +60,7 @@ def tile_pvconv2d_s_kernel(tc, x, Wk, bias, out):
         for k in range(1, POSITIONS):
             load_weights(k)
         bias_bf = small.tile([P, HALVES], BF16)
-        nc.scalar.dma_start(out=bias_bf, in_=bias.rearrange("(m h) -> m h", h=HALVES))
-
-        one = small.tile([P, 1], F32)
-        nc.vector.memset(one, 1.0)
-        neg_half = small.tile([P, 1], F32)
-        nc.vector.memset(neg_half, -0.5)
-        warm = small.tile([P, 1], F32)
-        nc.scalar.activation(out=warm, in_=one, func=ACT.Ln)
-        ident = keep.tile([P, P], F32)
-        make_identity(nc, ident)
+        nc.sync.dma_start(out=bias_bf, in_=bias.rearrange("(m h) -> m h", h=HALVES))
 
         zeros = keep.tile([P, PIXELS * PACK], BF16, align_bytes=64)
         nc.vector.memset(zeros.bitcast(I32), 0)
@@ -87,6 +78,15 @@ def tile_pvconv2d_s_kernel(tc, x, Wk, bias, out):
                 start=True,
                 stop=True,
             )
+
+        one = small.tile([P, 1], F32)
+        nc.vector.memset(one, 1.0)
+        neg_half = small.tile([P, 1], F32)
+        nc.vector.memset(neg_half, -0.5)
+        warm = small.tile([P, 1], F32)
+        nc.scalar.activation(out=warm, in_=one, func=ACT.Ln)
+        ident = keep.tile([P, P], F32)
+        make_identity(nc, ident)
 
         def keep_warm():
             unread = ps_misc.tile([P, P], F32, tag="misc")
@@ -120,14 +120,15 @@ def tile_pvconv2d_s_kernel(tc, x, Wk, bias, out):
 
         grouped_tiles = {}
 
-        def flip_and_regroup(k, copy=nc.scalar.copy):
+        def flip_and_regroup(k):
             words = w_rows[k].bitcast(F32)
-            flipped = ps_w.tile([P, HALVES * 2, P], F32, name="flipped")
-            for hu in range(HALVES * 2):
-                nc.tensor.transpose(flipped[:, hu, :], words[:, hu * P : (hu + 1) * P], ident)
-            grouped = w_stage.tile([P, HALVES, P, 2], F32, align_bytes=64, name="grouped")
-            copy(out=grouped, in_=flipped.rearrange("q (h u) m -> q h m u", u=2))
-            grouped_tiles[k] = grouped
+            flipped = ps_w.tile([P, HALVES, 2, P], F32, name="flipped")
+            for h in BOTH:
+                for u in range(2):
+                    word = (2 * h + u) * P
+                    nc.tensor.transpose(flipped[:, h, u, :], words[:, word : word + P], ident)
+            grouped_tiles[k] = w_stage.tile([P, HALVES, P, 2], F32, align_bytes=64, name="grouped")
+            nc.scalar.copy(out=grouped_tiles[k], in_=flipped.rearrange("q h u m -> q h m u"))
 
         def quantise_weights(k):
             nc.vector.quantize_mx(
@@ -138,8 +139,6 @@ def tile_pvconv2d_s_kernel(tc, x, Wk, bias, out):
 
         pre = keep.tile([P, CH_OUT + 1], F32)
         nc.vector.tensor_scalar_mul(out=pre[:, CH_OUT:], in0=one, scalar1=SQRT_C * EPS)
-        bias_f = small.tile([P, HALVES], F32)
-        nc.scalar.activation(out=bias_f, in_=bias_bf, func=ACT.Copy, scale=SQRT_C)
 
         flip_and_regroup(0)
 
@@ -154,7 +153,8 @@ def tile_pvconv2d_s_kernel(tc, x, Wk, bias, out):
             out=diagonal, in0=gram, scalar=EPS * EPS, in1=ident_4c, op0=ALU.add, op1=ALU.mult, accum_out=twice_z_sq
         )
         half_inv_z = inverse_root(twice_z_sq, "half_inv_z")
-        flip_and_regroup(1, nc.vector.tensor_copy)
+        quantise_weights(0)
+        flip_and_regroup(1)
         flip_and_regroup(2)
         keep_warm()
 
@@ -162,21 +162,22 @@ def tile_pvconv2d_s_kernel(tc, x, Wk, bias, out):
         nc.vector.tensor_scalar(
             out=twice_z, in0=twice_z_sq, scalar1=half_inv_z, scalar2=2 * (1.0 - 1e-6), op0=ALU.mult, op1=ALU.min
         )
-        quantise_weights(0)
         ln_plus = small.tile([P, 1], F32)
         nc.scalar.activation(out=ln_plus, in_=twice_z, func=ACT.Ln, bias=one, scale=0.5)
         ln_minus = small.tile([P, 1], F32)
         nc.scalar.activation(out=ln_minus, in_=twice_z, func=ACT.Ln, bias=one, scale=-0.5)
+        quantise_weights(1)
+
         factor = small.tile([P, 1], F32)
         nc.vector.tensor_scalar(
             out=factor, in0=ln_plus, scalar1=ln_minus, scalar2=half_inv_z, op0=ALU.subtract, op1=ALU.mult
         )
-        quantise_weights(1)
         flip_and_regroup(3)
         flip_and_regroup(4)
-        keep_warm()
         factor_all = spread(factor, ident)
+        keep_warm()
         flip_and_regroup(5)
+        quantise_weights(2)
         u_bf = keep.tile([P, PIXELS, PACK], BF16, align_bytes=64)
         u_by_batch = u_bf.rearrange("q (r b s) t -> q b r s t", r=ROWS, b=BATCH)
         x_by_batch = x_sb.rearrange("q t (b r s) -> q b r s t", b=BATCH, r=ROWS)
@@ -191,28 +192,31 @@ def tile_pvconv2d_s_kernel(tc, x, Wk, bias, out):
                 op=ALU.mult,
             )
         keep_warm()
+        bias_f = small.tile([P, HALVES], F32)
         for k in range(6, POSITIONS):
             flip_and_regroup(k)
+            if k == 6:
+                nc.scalar.activation(out=bias_f, in_=bias_bf, func=ACT.Copy, scale=SQRT_C)
 
-        quantise_weights(2)
+        quantise_weights(3)
         middle = 1
         nc.vector.quantize_mx(
             out=u_codes[:, middle, ROW_STEP : ROW_STEP + PIXELS].bitcast(FP8X4),
             scales=u_scales[:, middle, SCALE_PAD : SCALE_PAD + PIXELS],
             in_=u_bf.rearrange("q n t -> q (n t)"),
         )
-        quantise_weights(3)
+        quantise_weights(4)
         code_rows = u_codes[:, :, ROW_STEP : ROW_STEP + PIXELS].bitcast(I32).rearrange("q j (g s) -> q j g s", s=COLS)
         scale_rows = u_scales[:, :, SCALE_PAD : SCALE_PAD + PIXELS].rearrange("q j (g s) -> q j g s", s=COLS)
         for rows in (scale_rows, code_rows):
             nc.vector.tensor_copy(out=rows[:, 0, :, 1:COLS], in_=rows[:, middle, :, 0 : COLS - 1])
             nc.vector.tensor_copy(out=rows[:, 2, :, 0 : COLS - 1], in_=rows[:, middle, :, 1:COLS])
-        quantise_weights(4)
+        quantise_weights(5)
         words = u_scales.bitcast(I32)
         for moved, first in ((u_scales_up, SCALE_PAD - ROW_STEP), (u_scales_down, SCALE_PAD + ROW_STEP)):
             nc.vector.tensor_copy(out=moved.bitcast(I32), in_=words[:, :, first // 4 : (first + PIXELS) // 4])
         window_scales = (u_scales_up, u_scales[:, :, SCALE_PAD : SCALE_PAD + PIXELS], u_scales_down)
-        for k in range(5, POSITIONS):
+        for k in range(6, POSITIONS):
             quantise_weights(k)
 
         bias_ps = ps_misc.tile([P, HALVES, P], F32, tag="misc")
@@ -223,7 +227,8 @@ def tile_pvconv2d_s_kernel(tc, x, Wk, bias, out):
         nc.scalar.activation(out=warm, in_=one, func=ACT.Tanh)
 
         acc = ps_acc.tile([P, CH_OUT], F32)
-        for k in range(POSITIONS):
+        order = (4, 3, 5, 0, 1, 2, 6, 7, 8)
+        for k in order:
             i, j = divmod(k, TAPS)
             nc.tensor.matmul_mx(
                 out=acc,
@@ -231,8 +236,8 @@ def tile_pvconv2d_s_kernel(tc, x, Wk, bias, out):
                 lhsT_scale=window_scales[i][:, j, :],
                 rhs=w_codes[:, k, :].bitcast(FP8X4),
                 rhs_scale=w_scales[:, k, :],
-                start=(k == 0),
-                stop=(k == POSITIONS - 1),
+                start=(k == order[0]),
+                stop=(k == order[-1]),
             )
 
         nc.vector.scalar_tensor_tensor(

from concourse import mybir
from concourse.masks import make_identity

F32 = mybir.dt.float32
BF16 = mybir.dt.bfloat16
U8 = mybir.dt.uint8
U32 = mybir.dt.uint32
I32 = mybir.dt.int32
FP8X4 = mybir.dt.float8_e4m3fn_x4
ACT = mybir.ActivationFunctionType
ALU = mybir.AluOpType

P = 128
BATCH, CH_IN, CH_OUT, ROWS, COLS = 2, 512, 256, 8, 8
TAPS = 3
POSITIONS = TAPS * TAPS
IMAGE = ROWS * COLS
PIXELS = BATCH * IMAGE
PACK = 4
HALVES = CH_OUT // P
BOTH = range(HALVES)

ROW_STEP = BATCH * COLS
PLANE = (ROWS + 2) * ROW_STEP
SCALE_PAD = 64
SCALE_PLANE = PIXELS + 2 * SCALE_PAD
MX_WARM_UPS = 10

SQRT_C = 0.1
EPS = 1e-7
FLOPS = 2 * PIXELS * CH_IN * POSITIONS * CH_OUT


def tile_pvconv2d_s_kernel(tc, x, Wk, bias, out):
    nc = tc.nc
    with (
        tc.tile_pool(name="keep", bufs=1) as keep,
        tc.tile_pool(name="small", bufs=1) as small,
        tc.tile_pool(name="w_in", bufs=POSITIONS) as w_in,
        tc.tile_pool(name="w_stage", bufs=POSITIONS) as w_stage,
        tc.psum_pool(name="ps_w", bufs=4) as ps_w,
        tc.psum_pool(name="ps_acc", bufs=1) as ps_acc,
        tc.psum_pool(name="ps_misc", bufs=3) as ps_misc,
        tc.manual_schedule(),
    ):
        w_rows = []

        def load_weights(k):
            rows = w_in.tile([P, HALVES * CH_IN], BF16, name="w_rows")
            nc.sync.dma_start(out=rows, in_=Wk[k].rearrange("(m h) c -> m (h c)", h=HALVES))
            w_rows.append(rows)

        load_weights(0)
        x_sb = keep.tile([P, PACK, PIXELS], BF16)
        x_by_t = x.rearrange("b (u q e) r s -> u e q b (r s)", u=2, q=P, e=2)
        for t in range(PACK):
            nc.sync.dma_start(
                out=x_sb[:, t, :].rearrange("q (b p) -> q b p", b=BATCH), in_=x_by_t[t // 2, t % 2]
            )
        for k in range(1, POSITIONS):
            load_weights(k)
        bias_bf = small.tile([P, HALVES], BF16)
        nc.sync.dma_start(out=bias_bf, in_=bias.rearrange("(m h) -> m h", h=HALVES))

        zeros = keep.tile([P, PIXELS * PACK], BF16, align_bytes=64)
        nc.vector.memset(zeros.bitcast(I32), 0)
        zero_codes = keep.tile([P, PIXELS], U32, align_bytes=64)
        zero_scales = keep.tile([P, PIXELS], U8, align_bytes=64)
        nc.vector.quantize_mx(out=zero_codes.bitcast(FP8X4), scales=zero_scales, in_=zeros)
        unread = ps_misc.tile([P, P], F32, tag="misc")
        for n in range(MX_WARM_UPS):
            nc.tensor.matmul_mx(
                out=unread,
                lhsT=zero_codes.bitcast(FP8X4),
                lhsT_scale=zero_scales,
                rhs=zero_codes.bitcast(FP8X4),
                rhs_scale=zero_scales,
                start=True,
                stop=True,
            )

        one = small.tile([P, 1], F32)
        nc.vector.memset(one, 1.0)
        neg_half = small.tile([P, 1], F32)
        nc.vector.memset(neg_half, -0.5)
        warm = small.tile([P, 1], F32)
        nc.scalar.activation(out=warm, in_=one, func=ACT.Ln)
        ident = keep.tile([P, P], F32)
        make_identity(nc, ident)

        def keep_warm():
            unread = ps_misc.tile([P, P], F32, tag="misc")
            nc.tensor.matmul(out=unread, lhsT=ident, rhs=ident, start=True, stop=True)

        u_codes = keep.tile([P, TAPS, PLANE], U32, align_bytes=64)
        nc.vector.memset(u_codes.bitcast(I32), 0)
        u_scales = keep.tile([P, TAPS, SCALE_PLANE], U8, align_bytes=64)
        nc.vector.memset(u_scales.bitcast(I32), 0)
        ident_4c = keep.tile([P, P], F32)
        nc.vector.tensor_scalar_mul(out=ident_4c, in0=ident, scalar1=4 * SQRT_C * SQRT_C)
        ident_brs = keep.tile([P, PIXELS], F32)
        nc.vector.tensor_copy(
            out=ident_brs.rearrange("p (b r s) -> p b r s", b=BATCH, r=ROWS),
            in_=ident.rearrange("p (r b s) -> p b r s", r=ROWS, b=BATCH),
        )
        u_scales_up = keep.tile([P, TAPS, PIXELS], U8, align_bytes=64)
        u_scales_down = keep.tile([P, TAPS, PIXELS], U8, align_bytes=64)
        w_codes = keep.tile([P, POSITIONS, CH_OUT], U32, align_bytes=64)
        w_scales = keep.tile([P, POSITIONS, CH_OUT], U8, align_bytes=64)

        def spread(column, order):
            spread_ps = ps_misc.tile([P, P], F32, tag="misc", name="spread_ps")
            nc.tensor.transpose(spread_ps, column.to_broadcast([P, P]), order)
            return spread_ps

        def inverse_root(column, name):
            inverse = small.tile([P, 1], F32, name=name)
            nc.gpsimd.tensor_tensor(out=inverse, in0=column, in1=neg_half, op=ALU.pow)
            return inverse

        grouped_tiles = {}

        def flip_and_regroup(k):
            words = w_rows[k].bitcast(F32)
            flipped = ps_w.tile([P, HALVES, 2, P], F32, name="flipped")
            for h in BOTH:
                for u in range(2):
                    word = (2 * h + u) * P
                    nc.tensor.transpose(flipped[:, h, u, :], words[:, word : word + P], ident)
            grouped_tiles[k] = w_stage.tile([P, HALVES, P, 2], F32, align_bytes=64, name="grouped")
            nc.scalar.copy(out=grouped_tiles[k], in_=flipped.rearrange("q h u m -> q h m u"))

        def quantise_weights(k):
            nc.vector.quantize_mx(
                out=w_codes[:, k, :].bitcast(FP8X4),
                scales=w_scales[:, k, :],
                in_=grouped_tiles[k].rearrange("q h m u -> q (h m u)").bitcast(BF16),
            )

        pre = keep.tile([P, CH_OUT + 1], F32)
        nc.vector.tensor_scalar_mul(out=pre[:, CH_OUT:], in0=one, scalar1=SQRT_C * EPS)

        flip_and_regroup(0)

        gram = ps_misc.tile([P, PIXELS], F32, tag="misc")
        for t in range(PACK):
            nc.tensor.matmul(
                out=gram, lhsT=x_sb[:, t, :], rhs=x_sb[:, t, :], start=(t == 0), stop=(t == PACK - 1)
            )
        diagonal = keep.tile([P, PIXELS], F32)
        twice_z_sq = small.tile([P, 1], F32)
        nc.vector.scalar_tensor_tensor(
            out=diagonal, in0=gram, scalar=EPS * EPS, in1=ident_4c, op0=ALU.add, op1=ALU.mult, accum_out=twice_z_sq
        )
        half_inv_z = inverse_root(twice_z_sq, "half_inv_z")
        quantise_weights(0)
        flip_and_regroup(1)
        flip_and_regroup(2)
        keep_warm()

        twice_z = small.tile([P, 1], F32)
        nc.vector.tensor_scalar(
            out=twice_z, in0=twice_z_sq, scalar1=half_inv_z, scalar2=2 * (1.0 - 1e-6), op0=ALU.mult, op1=ALU.min
        )
        ln_plus = small.tile([P, 1], F32)
        nc.scalar.activation(out=ln_plus, in_=twice_z, func=ACT.Ln, bias=one, scale=0.5)
        ln_minus = small.tile([P, 1], F32)
        nc.scalar.activation(out=ln_minus, in_=twice_z, func=ACT.Ln, bias=one, scale=-0.5)
        quantise_weights(1)

        factor = small.tile([P, 1], F32)
        nc.vector.tensor_scalar(
            out=factor, in0=ln_plus, scalar1=ln_minus, scalar2=half_inv_z, op0=ALU.subtract, op1=ALU.mult
        )
        flip_and_regroup(3)
        flip_and_regroup(4)
        factor_all = spread(factor, ident)
        keep_warm()
        flip_and_regroup(5)
        quantise_weights(2)
        u_bf = keep.tile([P, PIXELS, PACK], BF16, align_bytes=64)
        u_by_batch = u_bf.rearrange("q (r b s) t -> q b r s t", r=ROWS, b=BATCH)
        x_by_batch = x_sb.rearrange("q t (b r s) -> q b r s t", b=BATCH, r=ROWS)
        for b in range(BATCH):
            nc.vector.tensor_tensor(
                out=u_by_batch[:, b],
                in0=x_by_batch[:, b],
                in1=factor_all[:, b * IMAGE : (b + 1) * IMAGE]
                .rearrange("q (r s) -> q r s", r=ROWS)
                .unsqueeze(3)
                .to_broadcast([P, ROWS, COLS, PACK]),
                op=ALU.mult,
            )
        keep_warm()
        bias_f = small.tile([P, HALVES], F32)
        for k in range(6, POSITIONS):
            flip_and_regroup(k)
            if k == 6:
                nc.scalar.activation(out=bias_f, in_=bias_bf, func=ACT.Copy, scale=SQRT_C)

        quantise_weights(3)
        middle = 1
        nc.vector.quantize_mx(
            out=u_codes[:, middle, ROW_STEP : ROW_STEP + PIXELS].bitcast(FP8X4),
            scales=u_scales[:, middle, SCALE_PAD : SCALE_PAD + PIXELS],
            in_=u_bf.rearrange("q n t -> q (n t)"),
        )
        quantise_weights(4)
        code_rows = u_codes[:, :, ROW_STEP : ROW_STEP + PIXELS].bitcast(I32).rearrange("q j (g s) -> q j g s", s=COLS)
        scale_rows = u_scales[:, :, SCALE_PAD : SCALE_PAD + PIXELS].rearrange("q j (g s) -> q j g s", s=COLS)
        for rows in (scale_rows, code_rows):
            nc.vector.tensor_copy(out=rows[:, 0, :, 1:COLS], in_=rows[:, middle, :, 0 : COLS - 1])
            nc.vector.tensor_copy(out=rows[:, 2, :, 0 : COLS - 1], in_=rows[:, middle, :, 1:COLS])
        quantise_weights(5)
        words = u_scales.bitcast(I32)
        for moved, first in ((u_scales_up, SCALE_PAD - ROW_STEP), (u_scales_down, SCALE_PAD + ROW_STEP)):
            nc.vector.tensor_copy(out=moved.bitcast(I32), in_=words[:, :, first // 4 : (first + PIXELS) // 4])
        window_scales = (u_scales_up, u_scales[:, :, SCALE_PAD : SCALE_PAD + PIXELS], u_scales_down)
        for k in range(6, POSITIONS):
            quantise_weights(k)

        bias_ps = ps_misc.tile([P, HALVES, P], F32, tag="misc")
        for h in BOTH:
            nc.tensor.transpose(bias_ps[:, h, :], bias_f[:, h : h + 1].to_broadcast([P, P]), ident)
        bias_all = keep.tile([P, HALVES, P], F32)
        nc.scalar.copy(out=bias_all, in_=bias_ps)
        nc.scalar.activation(out=warm, in_=one, func=ACT.Tanh)

        acc = ps_acc.tile([P, CH_OUT], F32)
        order = (4, 3, 5, 0, 1, 2, 6, 7, 8)
        for k in order:
            i, j = divmod(k, TAPS)
            nc.tensor.matmul_mx(
                out=acc,
                lhsT=u_codes[:, j, i * ROW_STEP : i * ROW_STEP + PIXELS].bitcast(FP8X4),
                lhsT_scale=window_scales[i][:, j, :],
                rhs=w_codes[:, k, :].bitcast(FP8X4),
                rhs_scale=w_scales[:, k, :],
                start=(k == order[0]),
                stop=(k == order[-1]),
            )

        nc.vector.scalar_tensor_tensor(
            out=pre[:, 0:CH_OUT], in0=acc, scalar=SQRT_C, in1=bias_all.rearrange("q h m -> q (h m)"), op0=ALU.mult, op1=ALU.add
        )
        back = ps_misc.tile([P, HALVES, PIXELS], F32, tag="misc")
        for h in BOTH:
            nc.tensor.transpose(back[:, h, :], pre[:, h * P : (h + 1) * P], ident_brs)
        relu = keep.tile([P, HALVES, PIXELS], F32)
        nc.scalar.activation(out=relu, in_=back, func=ACT.Relu, scale=1.0 / SQRT_C)
        relu_sq = keep.tile([P, CH_OUT + 1], F32)
        y_sq = small.tile([P, 1], F32)
        nc.vector.scalar_tensor_tensor(
            out=relu_sq, in0=pre, scalar=0.0, in1=pre, op0=ALU.max, op1=ALU.mult, accum_out=y_sq
        )
        inv_y = inverse_root(y_sq, "inv_y")
        tanh_y = small.tile([P, 1], F32)
        nc.scalar.activation(out=tanh_y, in_=y_sq, func=ACT.Tanh, scale=inv_y)
        gain = small.tile([P, 1], F32)
        nc.scalar.activation(out=gain, in_=tanh_y, func=ACT.Copy, scale=inv_y)
        gain_all = spread(gain, ident_brs)
        out_sb = keep.tile([P, BATCH, HALVES, IMAGE], F32)
        nc.vector.tensor_tensor(
            out=out_sb,
            in0=relu.rearrange("m h (b p) -> m b h p", b=BATCH),
            in1=gain_all.rearrange("m (b p) -> m b p", b=BATCH).unsqueeze(2).to_broadcast([P, BATCH, HALVES, IMAGE]),
            op=ALU.mult,
        )
        nc.sync.dma_start(
            out=out.rearrange("b (m h) r s -> m b (h r s)", h=HALVES),
            in_=out_sb.rearrange("m b h p -> m b (h p)"),
        )
